import numpy as np
import ml_dtypes


def mxq(x, axis, fmt="e4m3"):
    dtype, down = {"e4m3": (ml_dtypes.float8_e4m3fn, 7), "e5m2": (ml_dtypes.float8_e5m2, 14)}[fmt]
    v = np.moveaxis(np.asarray(x, np.float32).astype(ml_dtypes.bfloat16).astype(np.float64), axis, -1)
    blocks = v.reshape(v.shape[:-1] + (-1, 32))
    amax = np.abs(blocks).max(-1, keepdims=True)
    byte = np.maximum(np.where(amax > 0, np.frexp(amax)[1] - 1 + 127, 0) - down, 1)
    scale = np.exp2(byte - 127.0)
    codes = (blocks / scale).astype(np.float32).astype(dtype).astype(np.float64)
    return np.moveaxis((codes * scale).reshape(v.shape), -1, axis)


WIDE = False


def mx_kscale(k):
    if not WIDE:
        return np.ones(k)
    levels = np.array([10, -10, 5, -5, 0])
    a = np.random.permutation(np.resize(levels, k // 512 * 4)).reshape(k // 512, 4)
    idx = np.arange(k)
    return np.exp2(a[idx // 512, idx % 128 // 32])


BF16 = ml_dtypes.bfloat16


def bf(x):
    return np.asarray(x, np.float32).astype(BF16)


def f64(x):
    return np.asarray(x).astype(np.float64)


E2M1 = np.array([0.0, 0.5, 1.0, 1.5, 2.0, 3.0, 4.0, 6.0, -0.0, -0.5, -1.0, -1.5, -2.0, -3.0, -4.0, -6.0])


def pack_weight(w, fmt):
    k, n = w.shape
    w = f64(bf(w)).reshape(k // 32, 32, n)
    amax = np.abs(w).max(1)
    if fmt == "e4m3":
        byte = np.frexp(amax)[1] - 1 + 127 - 7
    else:
        mant, ex = np.frexp(amax / 6.0)
        byte = np.where(mant > 0.5, ex, ex - 1) + 127
    byte = np.clip(np.where(amax > 0, byte, 1), 1, 254)
    scaled = (w * np.exp2(127.0 - byte)[:, None, :]).reshape(k, n).astype(np.float32)
    by_word = np.ascontiguousarray(scaled.reshape(k // 512, 128, 4, n).transpose(0, 1, 3, 2))
    if fmt == "e4m3":
        words = by_word.astype(ml_dtypes.float8_e4m3fn).view(np.uint8)
    else:
        c = by_word.astype(ml_dtypes.float4_e2m1fn).view(np.uint8) & 0xF
        words = c[..., 0::2] | (c[..., 1::2] << 4)
    return np.ascontiguousarray(words), np.ascontiguousarray(byte.astype(np.uint8).reshape(k // 512, 16, n))


def unpack_weight(words, scales, fmt):
    g, p, n, _ = words.shape
    if fmt == "e4m3":
        vals = np.ascontiguousarray(words).view(ml_dtypes.float8_e4m3fn).astype(np.float64)
    else:
        nib = np.empty((g, p, n, 4), np.uint8)
        nib[..., 0::2] = words & 0xF
        nib[..., 1::2] = words >> 4
        vals = E2M1[nib]
    vals = vals * np.repeat(np.exp2(scales.astype(np.float64) - 127.0), 8, axis=1)[..., None]
    return vals.transpose(0, 1, 3, 2).reshape(g * 512, n)


N, C, D, H, W = 2, 16, 512, 16, 16
EPS = 1e-5


def setup_inputs():
    t = np.minimum(mx_kscale(D), 1.0) ** 2
    sig0 = 0.01 * (0.5 + np.random.random_sample((C, D)))
    sig = sig0 * t
    r = np.exp2(np.round(np.log2((sig / np.sqrt(sig**2 + EPS)) / (sig0 / np.sqrt(sig0**2 + EPS)))))
    mu = np.random.standard_normal((C, D))
    z = np.random.standard_normal((N, C, D, H, W))
    x = ((z + mu[None, :, :, None, None]) * sig[None, :, :, None, None]).reshape(N, C * D, H, W)
    weight = (np.eye(D)[None] + np.random.standard_normal((C, D, D)) / np.sqrt(D)) / r[:, None, :]
    cat = np.ascontiguousarray(np.swapaxes(weight, 1, 2)).reshape(-1, D)
    words, scales = pack_weight(cat, "e4m3")
    return {"x": bf(x), "weight_words": words, "weight_scales": scales, "bias": bf(np.random.standard_normal(C * D) * 0.3)}


def reference(x, weight_words, weight_scales, bias):
    x, bias = f64(x), f64(bias)
    n, cd, h, w = x.shape
    c = C
    d = cd // c
    mean = np.mean(x, axis=(0, 2, 3), keepdims=True)
    var = np.mean(np.square(x - mean), axis=(0, 2, 3), keepdims=True)
    xn = (x - mean) / np.sqrt(var + EPS)
    xg = xn.reshape(n, c, d, h * w)
    out = unpack_weight(weight_words, weight_scales, "e4m3").reshape(C, D, D).swapaxes(1, 2)[None] @ mxq(xg, 2, "e4m3")
    return out.reshape(n, cd, h, w) + bias[None, :, None, None]

@@ -1,0 +1,158 @@
+from contextlib import ExitStack
+
+import concourse.mybir as mybir
+from concourse.masks import make_identity
+
+F32 = mybir.dt.float32
+BF16 = mybir.dt.bfloat16
+I32 = mybir.dt.int32
+U32 = mybir.dt.uint32
+U8 = mybir.dt.uint8
+FP8X4 = mybir.dt.float8_e4m3fn_x4
+ALU = mybir.AluOpType
+ACT = mybir.ActivationFunctionType
+
+P = 128
+PACK = 4
+BATCH = 2
+CAPS = 16
+CH = P * PACK
+PIX = 256
+COLS = BATCH * PIX
+M_TILES = CH // P
+EPS = 1e-5
+STATS = 6
+AHEAD = 2
+
+FLOPS = 2 * CAPS * CH * CH * COLS
+
+
+def tile_caps_bn_e_kernel(tc, x, weight_words, weight_scales, bias, out):
+    nc = tc.nc
+
+    x_view = x.rearrange("n (c p t) h w -> c p n (t h w)", c=CAPS, p=P, t=PACK)
+    out_view = out.rearrange("n (c m p) h w -> c m p n (h w)", c=CAPS, m=M_TILES, p=P)
+
+    with ExitStack() as ctx:
+        keep = ctx.enter_context(tc.tile_pool(name="keep", bufs=1))
+        small = ctx.enter_context(tc.tile_pool(name="small", bufs=AHEAD + 2))
+        work = ctx.enter_context(tc.tile_pool(name="work", bufs=2))
+        results = ctx.enter_context(tc.tile_pool(name="results", bufs=24))
+        psum_once = ctx.enter_context(tc.psum_pool(name="psum_once", bufs=1))
+        psum = ctx.enter_context(tc.psum_pool(name="psum", bufs=6))
+
+        x_all = keep.tile([P, CAPS, BATCH, PACK, PIX], BF16)
+        w_codes = keep.tile([P, CAPS, CH], I32, align_bytes=64)
+        w_planes = keep.tile([P, CAPS, CH], U8, align_bytes=64)
+        bias_rows = keep.tile([P, P], BF16)
+        identity = keep.tile([P, P], BF16)
+        bias_cols = keep.tile([P, CAPS * M_TILES], F32)
+        minus_half = keep.tile([P, PACK], F32)
+
+        nc.vector.memset(w_planes[:].rearrange("p g n -> p (g n)").bitcast(I32), 0)
+        nc.vector.memset(minus_half[:], -0.5)
+        nc.vector.memset(bias_rows[:], 0.0)
+        make_identity(nc, identity[:])
+
+        def load_x(c):
+            nc.sync.dma_start(out=x_all[:, c].rearrange("p n t f -> p n (t f)"), in_=x_view[c])
+
+        def load_w(c):
+            nc.sync.dma_start(
+                out=w_codes[:, c, :],
+                in_=weight_words[c].rearrange("p n t -> p (n t)").bitcast(I32),
+            )
+
+        nc.scalar.dma_start(out=bias_rows[0 : CAPS * M_TILES, :], in_=bias.rearrange("(r p) -> r p", p=P))
+        for c in range(AHEAD):
+            load_x(c)
+        scale_rows = weight_scales.rearrange("g (Q r) n -> r Q g n", r=PACK)
+        for r in range(PACK):
+            nc.sync.dma_start(out=w_planes[r:P:32, :, :].bitcast(I32), in_=scale_rows[r].bitcast(I32))
+        for c in range(CAPS):
+            load_w(c)
+            if c + AHEAD < CAPS:
+                load_x(c + AHEAD)
+
+        bias_ps = psum_once.tile([P, P], BF16)
+        nc.tensor.transpose(bias_ps[:], bias_rows[:], identity[:])
+        nc.scalar.copy(out=bias_cols[:], in_=bias_ps[:, 0 : CAPS * M_TILES])
+
+        mean_var = {}
+        rstd = {}
+        grouped = {}
+        codes = {}
+        planes = {}
+
+        def statistics(c):
+            stats = small.tile([P, PACK, STATS], F32, name="stats")
+            mean_var[c] = small.tile([P, PACK, 2], F32, name="mean_var")
+            var_eps = small.tile([P, PACK], F32, name="var_eps")
+            rstd[c] = small.tile([P, PACK], F32, name="rstd")
+            for t in range(PACK):
+                nc.vector.bn_stats(out=stats[:, t, :], in_=x_all[:, c, :, t, :])
+            for t in range(PACK):
+                nc.vector.bn_aggr(out=mean_var[c][:, t, :], in_=stats[:, t, :])
+            nc.gpsimd.tensor_scalar(
+                out=var_eps[:], in0=mean_var[c][:, :, 1], scalar1=1.0, scalar2=EPS, op0=ALU.mult, op1=ALU.add
+            )
+            nc.gpsimd.tensor_tensor(out=rstd[c][:], in0=var_eps[:], in1=minus_half[:], op=ALU.pow)
+
+        def normalise_and_regroup(c):
+            xn = work.tile([P, PACK, COLS], BF16, name="xn")
+            for t in range(PACK):
+                nc.vector.tensor_scalar(
+                    out=xn[:, t, :].rearrange("p (n f) -> p n f", n=BATCH),
+                    in0=x_all[:, c, :, t, :],
+                    scalar1=mean_var[c][:, t, 0:1],
+                    scalar2=rstd[c][:, t : t + 1],
+                    op0=ALU.subtract,
+                    op1=ALU.mult,
+                )
+            grouped[c] = work.tile([P, COLS, PACK], BF16, name="grouped", align_bytes=64)
+            nc.vector.tensor_copy(
+                out=grouped[c][:, 0:PIX, :].rearrange("p (c i) t -> p c t i", i=4),
+                in_=xn[:, :, 0:PIX].rearrange("p t (c i) -> p c t i", i=4),
+            )
+            nc.scalar.copy(
+                out=grouped[c][:, PIX:COLS, :].rearrange("p (c i) t -> p c t i", i=4),
+                in_=xn[:, :, PIX:COLS].rearrange("p t (c i) -> p c t i", i=4),
+            )
+
+        def quantise(c):
+            codes[c] = work.tile([P, COLS], U32, name="codes", align_bytes=64)
+            planes[c] = work.tile([P, COLS], U8, name="planes", align_bytes=64)
+            nc.vector.quantize_mx(
+                out=codes[c][:].bitcast(FP8X4),
+                scales=planes[c][:],
+                in_=grouped[c][:].rearrange("p c t -> p (c t)"),
+            )
+
+        def multiply_and_store(c):
+            for m in range(M_TILES):
+                o_cols = slice(m * P, (m + 1) * P)
+                acc = psum.tile([P, COLS], F32, name="acc")
+                nc.tensor.matmul_mx(
+                    out=acc[:],
+                    lhsT=w_codes[:, c, o_cols].bitcast(FP8X4),
+                    lhsT_scale=w_planes[:, c, o_cols],
+                    rhs=codes[c][:].bitcast(FP8X4),
+                    rhs_scale=planes[c][:],
+                    start=True,
+                    stop=True,
+                )
+                result = results.tile([P, COLS], F32, name="result")
+                r = c * M_TILES + m
+                nc.scalar.activation(out=result[:], in_=acc[:], func=ACT.Identity, bias=bias_cols[:, r : r + 1])
+                nc.sync.dma_start(out=out_view[c, m], in_=result[:].rearrange("p (n f) -> p n f", n=BATCH))
+
+        for c in range(AHEAD):
+            statistics(c)
+        for c in range(CAPS):
+            normalise_and_regroup(c)
+            if c >= 1:
+                multiply_and_store(c - 1)
+            if c + AHEAD < CAPS:
+                statistics(c + AHEAD)
+            quantise(c)
+        multiply_and_store(CAPS - 1)

@@ -22,7 +22,7 @@ COLS = BATCH * PIX
 M_TILES = CH // P
 EPS = 1e-5
 STATS = 6
-AHEAD = 2
+AHEAD = 3
 
 FLOPS = 2 * CAPS * CH * CH * COLS
 
@@ -34,8 +34,9 @@ def tile_caps_bn_e_kernel(tc, x, weight_words, weight_scales, bias, out):
     out_view = out.rearrange("n (c m p) h w -> c m p n (h w)", c=CAPS, m=M_TILES, p=P)
 
     with ExitStack() as ctx:
+        ctx.enter_context(tc.manual_schedule())
         keep = ctx.enter_context(tc.tile_pool(name="keep", bufs=1))
-        small = ctx.enter_context(tc.tile_pool(name="small", bufs=AHEAD + 2))
+        small = ctx.enter_context(tc.tile_pool(name="small", bufs=AHEAD + 1))
         work = ctx.enter_context(tc.tile_pool(name="work", bufs=2))
         results = ctx.enter_context(tc.tile_pool(name="results", bufs=24))
         psum_once = ctx.enter_context(tc.psum_pool(name="psum_once", bufs=1))
@@ -78,21 +79,24 @@ def tile_caps_bn_e_kernel(tc, x, weight_words, weight_scales, bias, out):
         nc.tensor.transpose(bias_ps[:], bias_rows[:], identity[:])
         nc.scalar.copy(out=bias_cols[:], in_=bias_ps[:, 0 : CAPS * M_TILES])
 
+        stats = {}
         mean_var = {}
         rstd = {}
         grouped = {}
         codes = {}
         planes = {}
 
-        def statistics(c):
-            stats = small.tile([P, PACK, STATS], F32, name="stats")
+        def partial_statistics(c):
+            stats[c] = small.tile([P, PACK, STATS], F32, name="stats")
+            for t in range(PACK):
+                nc.vector.bn_stats(out=stats[c][:, t, :], in_=x_all[:, c, :, t, :])
+
+        def mean_and_rstd(c):
             mean_var[c] = small.tile([P, PACK, 2], F32, name="mean_var")
             var_eps = small.tile([P, PACK], F32, name="var_eps")
             rstd[c] = small.tile([P, PACK], F32, name="rstd")
             for t in range(PACK):
-                nc.vector.bn_stats(out=stats[:, t, :], in_=x_all[:, c, :, t, :])
-            for t in range(PACK):
-                nc.vector.bn_aggr(out=mean_var[c][:, t, :], in_=stats[:, t, :])
+                nc.vector.bn_aggr(out=mean_var[c][:, t, :], in_=stats[c][:, t, :])
             nc.gpsimd.tensor_scalar(
                 out=var_eps[:], in0=mean_var[c][:, :, 1], scalar1=1.0, scalar2=EPS, op0=ALU.mult, op1=ALU.add
             )
@@ -128,7 +132,7 @@ def tile_caps_bn_e_kernel(tc, x, weight_words, weight_scales, bias, out):
                 in_=grouped[c][:].rearrange("p c t -> p (c t)"),
             )
 
-        def multiply_and_store(c):
+        def multiply_and_store(c, vector_is_idle):
             for m in range(M_TILES):
                 o_cols = slice(m * P, (m + 1) * P)
                 acc = psum.tile([P, COLS], F32, name="acc")
@@ -143,16 +147,23 @@ def tile_caps_bn_e_kernel(tc, x, weight_words, weight_scales, bias, out):
                 )
                 result = results.tile([P, COLS], F32, name="result")
                 r = c * M_TILES + m
-                nc.scalar.activation(out=result[:], in_=acc[:], func=ACT.Identity, bias=bias_cols[:, r : r + 1])
+                if vector_is_idle and m % 2 == 1:
+                    nc.vector.tensor_scalar_add(out=result[:], in0=acc[:], scalar1=bias_cols[:, r : r + 1])
+                else:
+                    nc.scalar.activation(out=result[:], in_=acc[:], func=ACT.Identity, bias=bias_cols[:, r : r + 1])
                 nc.sync.dma_start(out=out_view[c, m], in_=result[:].rearrange("p (n f) -> p n f", n=BATCH))
 
         for c in range(AHEAD):
-            statistics(c)
+            partial_statistics(c)
+            if c + 1 < AHEAD:
+                mean_and_rstd(c)
         for c in range(CAPS):
             normalise_and_regroup(c)
             if c >= 1:
-                multiply_and_store(c - 1)
+                multiply_and_store(c - 1, vector_is_idle=False)
+            if c + AHEAD - 1 < CAPS:
+                mean_and_rstd(c + AHEAD - 1)
             if c + AHEAD < CAPS:
-                statistics(c + AHEAD)
+                partial_statistics(c + AHEAD)
             quantise(c)
-        multiply_and_store(CAPS - 1)
+        multiply_and_store(CAPS - 1, vector_is_idle=True)

@@ -22,7 +22,6 @@ COLS = BATCH * PIX
 M_TILES = CH // P
 EPS = 1e-5
 STATS = 6
-AHEAD = 3
 
 FLOPS = 2 * CAPS * CH * CH * COLS
 
@@ -36,7 +35,7 @@ def tile_caps_bn_e_kernel(tc, x, weight_words, weight_scales, bias, out):
     with ExitStack() as ctx:
         ctx.enter_context(tc.manual_schedule())
         keep = ctx.enter_context(tc.tile_pool(name="keep", bufs=1))
-        small = ctx.enter_context(tc.tile_pool(name="small", bufs=AHEAD + 1))
+        small = ctx.enter_context(tc.tile_pool(name="small", bufs=4))
         work = ctx.enter_context(tc.tile_pool(name="work", bufs=2))
         results = ctx.enter_context(tc.tile_pool(name="results", bufs=24))
         psum_once = ctx.enter_context(tc.psum_pool(name="psum_once", bufs=1))
@@ -48,11 +47,13 @@ def tile_caps_bn_e_kernel(tc, x, weight_words, weight_scales, bias, out):
         bias_rows = keep.tile([P, P], BF16)
         identity = keep.tile([P, P], BF16)
         bias_cols = keep.tile([P, CAPS * M_TILES], F32)
-        minus_half = keep.tile([P, PACK], F32)
+        zero_col = keep.tile([P, 1], F32)
+        eps_col = keep.tile([P, 1], F32)
 
         nc.vector.memset(w_planes[:].rearrange("p g n -> p (g n)").bitcast(I32), 0)
-        nc.vector.memset(minus_half[:], -0.5)
         nc.vector.memset(bias_rows[:], 0.0)
+        nc.vector.memset(zero_col[:], 0.0)
+        nc.vector.tensor_scalar_add(out=eps_col[:], in0=zero_col[:], scalar1=EPS)
         make_identity(nc, identity[:])
 
         def load_x(c):
@@ -65,15 +66,15 @@ def tile_caps_bn_e_kernel(tc, x, weight_words, weight_scales, bias, out):
             )
 
         nc.scalar.dma_start(out=bias_rows[0 : CAPS * M_TILES, :], in_=bias.rearrange("(r p) -> r p", p=P))
-        for c in range(AHEAD):
-            load_x(c)
+        load_x(0)
+        load_x(1)
         scale_rows = weight_scales.rearrange("g (Q r) n -> r Q g n", r=PACK)
         for r in range(PACK):
             nc.sync.dma_start(out=w_planes[r:P:32, :, :].bitcast(I32), in_=scale_rows[r].bitcast(I32))
         for c in range(CAPS):
             load_w(c)
-            if c + AHEAD < CAPS:
-                load_x(c + AHEAD)
+            if c + 2 < CAPS:
+                load_x(c + 2)
 
         bias_ps = psum_once.tile([P, P], BF16)
         nc.tensor.transpose(bias_ps[:], bias_rows[:], identity[:])
@@ -81,7 +82,9 @@ def tile_caps_bn_e_kernel(tc, x, weight_words, weight_scales, bias, out):
 
         stats = {}
         mean_var = {}
+        std = {}
         rstd = {}
+        xn = {}
         grouped = {}
         codes = {}
         planes = {}
@@ -91,22 +94,22 @@ def tile_caps_bn_e_kernel(tc, x, weight_words, weight_scales, bias, out):
             for t in range(PACK):
                 nc.vector.bn_stats(out=stats[c][:, t, :], in_=x_all[:, c, :, t, :])
 
-        def mean_and_rstd(c):
+        def mean_and_std(c):
             mean_var[c] = small.tile([P, PACK, 2], F32, name="mean_var")
-            var_eps = small.tile([P, PACK], F32, name="var_eps")
-            rstd[c] = small.tile([P, PACK], F32, name="rstd")
+            std[c] = small.tile([P, PACK], F32, name="std")
             for t in range(PACK):
                 nc.vector.bn_aggr(out=mean_var[c][:, t, :], in_=stats[c][:, t, :])
-            nc.gpsimd.tensor_scalar(
-                out=var_eps[:], in0=mean_var[c][:, :, 1], scalar1=1.0, scalar2=EPS, op0=ALU.mult, op1=ALU.add
-            )
-            nc.gpsimd.tensor_tensor(out=rstd[c][:], in0=var_eps[:], in1=minus_half[:], op=ALU.pow)
+            nc.scalar.activation(out=std[c][:], in_=mean_var[c][:, :, 1], func=ACT.Sqrt, bias=eps_col[:])
 
-        def normalise_and_regroup(c):
-            xn = work.tile([P, PACK, COLS], BF16, name="xn")
+        def invert_std(c):
+            rstd[c] = small.tile([P, PACK], F32, name="rstd")
+            nc.vector.reciprocal(out=rstd[c][:], in_=std[c][:])
+
+        def normalise(c):
+            xn[c] = work.tile([P, PACK, COLS], BF16, name="xn")
             for t in range(PACK):
                 nc.vector.tensor_scalar(
-                    out=xn[:, t, :].rearrange("p (n f) -> p n f", n=BATCH),
+                    out=xn[c][:, t, :].rearrange("p (n f) -> p n f", n=BATCH),
                     in0=x_all[:, c, :, t, :],
                     scalar1=mean_var[c][:, t, 0:1],
                     scalar2=rstd[c][:, t : t + 1],
@@ -114,13 +117,19 @@ def tile_caps_bn_e_kernel(tc, x, weight_words, weight_scales, bias, out):
                     op1=ALU.mult,
                 )
             grouped[c] = work.tile([P, COLS, PACK], BF16, name="grouped", align_bytes=64)
-            nc.vector.tensor_copy(
-                out=grouped[c][:, 0:PIX, :].rearrange("p (c i) t -> p c t i", i=4),
-                in_=xn[:, :, 0:PIX].rearrange("p t (c i) -> p c t i", i=4),
-            )
+
+        def regroup(c):
             nc.scalar.copy(
-                out=grouped[c][:, PIX:COLS, :].rearrange("p (c i) t -> p c t i", i=4),
-                in_=xn[:, :, PIX:COLS].rearrange("p t (c i) -> p c t i", i=4),
+                out=grouped[c][:, 0:PIX, :].rearrange("p (c i) t -> p c t i", i=4),
+                in_=xn[c][:, :, 0:PIX].rearrange("p t (c i) -> p c t i", i=4),
+            )
+            nc.gpsimd.tensor_scalar(
+                out=grouped[c][:, PIX:COLS, :],
+                in0=xn[c][:, :, PIX:COLS].rearrange("p t c -> p c t"),
+                scalar1=1.0,
+                scalar2=0.0,
+                op0=ALU.mult,
+                op1=ALU.add,
             )
 
         def quantise(c):
@@ -153,17 +162,20 @@ def tile_caps_bn_e_kernel(tc, x, weight_words, weight_scales, bias, out):
                     nc.scalar.activation(out=result[:], in_=acc[:], func=ACT.Identity, bias=bias_cols[:, r : r + 1])
                 nc.sync.dma_start(out=out_view[c, m], in_=result[:].rearrange("p (n f) -> p n f", n=BATCH))
 
-        for c in range(AHEAD):
-            partial_statistics(c)
-            if c + 1 < AHEAD:
-                mean_and_rstd(c)
+        partial_statistics(0)
+        mean_and_std(0)
+        partial_statistics(1)
+        invert_std(0)
         for c in range(CAPS):
-            normalise_and_regroup(c)
+            normalise(c)
+            regroup(c)
+            if c + 1 < CAPS:
+                mean_and_std(c + 1)
             if c >= 1:
                 multiply_and_store(c - 1, vector_is_idle=False)
-            if c + AHEAD - 1 < CAPS:
-                mean_and_rstd(c + AHEAD - 1)
-            if c + AHEAD < CAPS:
-                partial_statistics(c + AHEAD)
+            if c + 2 < CAPS:
+                partial_statistics(c + 2)
+            if c + 1 < CAPS:
+                invert_std(c + 1)
             quantise(c)
         multiply_and_store(CAPS - 1, vector_is_idle=True)

@@ -22,6 +22,7 @@ COLS = BATCH * PIX
 M_TILES = CH // P
 EPS = 1e-5
 STATS = 6
+SHARE = 4
 
 FLOPS = 2 * CAPS * CH * CH * COLS
 
@@ -43,7 +44,7 @@ def tile_caps_bn_e_kernel(tc, x, weight_words, weight_scales, bias, out):
 
         x_all = keep.tile([P, CAPS, BATCH, PACK, PIX], BF16)
         w_codes = keep.tile([P, CAPS, CH], I32, align_bytes=64)
-        w_planes = keep.tile([P, CAPS, CH], U8, align_bytes=64)
+        w_planes = keep.tile([P, CAPS // SHARE, CH], U8, align_bytes=64)
         bias_rows = keep.tile([P, P], BF16)
         identity = keep.tile([P, P], BF16)
         bias_cols = keep.tile([P, CAPS * M_TILES], F32)
@@ -65,13 +66,19 @@ def tile_caps_bn_e_kernel(tc, x, weight_words, weight_scales, bias, out):
                 in_=weight_words[c].rearrange("p n t -> p (n t)").bitcast(I32),
             )
 
+        def load_w_scales(s):
+            for Q in range(4):
+                nc.sync.dma_start(
+                    out=w_planes[32 * Q : 32 * Q + 4 * SHARE, s, :].bitcast(I32),
+                    in_=weight_scales[SHARE * s : SHARE * (s + 1), 4 * Q : 4 * Q + 4, :].bitcast(I32),
+                )
+
         nc.scalar.dma_start(out=bias_rows[0 : CAPS * M_TILES, :], in_=bias.rearrange("(r p) -> r p", p=P))
         load_x(0)
         load_x(1)
-        scale_rows = weight_scales.rearrange("g (Q r) n -> r Q g n", r=PACK)
-        for r in range(PACK):
-            nc.sync.dma_start(out=w_planes[r:P:32, :, :].bitcast(I32), in_=scale_rows[r].bitcast(I32))
         for c in range(CAPS):
+            if c % SHARE == 0:
+                load_w_scales(c // SHARE)
             load_w(c)
             if c + 2 < CAPS:
                 load_x(c + 2)
@@ -148,7 +155,7 @@ def tile_caps_bn_e_kernel(tc, x, weight_words, weight_scales, bias, out):
                 nc.tensor.matmul_mx(
                     out=acc[:],
                     lhsT=w_codes[:, c, o_cols].bitcast(FP8X4),
-                    lhsT_scale=w_planes[:, c, o_cols],
+                    lhsT_scale=w_planes[4 * (c % SHARE) : P, c // SHARE, o_cols],
                     rhs=codes[c][:].bitcast(FP8X4),
                     rhs_scale=planes[c][:],
                     start=True,

@@ -89,7 +89,6 @@ def tile_caps_bn_e_kernel(tc, x, weight_words, weight_scales, bias, out):
 
         stats = {}
         mean_var = {}
-        std = {}
         rstd = {}
         xn = {}
         grouped = {}
@@ -101,16 +100,14 @@ def tile_caps_bn_e_kernel(tc, x, weight_words, weight_scales, bias, out):
             for t in range(PACK):
                 nc.vector.bn_stats(out=stats[c][:, t, :], in_=x_all[:, c, :, t, :])
 
-        def mean_and_std(c):
+        def mean_and_rstd(c):
             mean_var[c] = small.tile([P, PACK, 2], F32, name="mean_var")
-            std[c] = small.tile([P, PACK], F32, name="std")
+            rstd[c] = small.tile([P, PACK], F32, name="rstd")
             for t in range(PACK):
                 nc.vector.bn_aggr(out=mean_var[c][:, t, :], in_=stats[c][:, t, :])
-            nc.scalar.activation(out=std[c][:], in_=mean_var[c][:, :, 1], func=ACT.Sqrt, bias=eps_col[:])
-
-        def invert_std(c):
-            rstd[c] = small.tile([P, PACK], F32, name="rstd")
-            nc.vector.reciprocal(out=rstd[c][:], in_=std[c][:])
+            nc.scalar.activation(
+                out=rstd[c][:], in_=mean_var[c][:, :, 1], func=ACT.Abs_reciprocal_sqrt, bias=eps_col[:]
+            )
 
         def normalise(c):
             xn[c] = work.tile([P, PACK, COLS], BF16, name="xn")
@@ -170,19 +167,16 @@ def tile_caps_bn_e_kernel(tc, x, weight_words, weight_scales, bias, out):
                 nc.sync.dma_start(out=out_view[c, m], in_=result[:].rearrange("p (n f) -> p n f", n=BATCH))
 
         partial_statistics(0)
-        mean_and_std(0)
+        mean_and_rstd(0)
         partial_statistics(1)
-        invert_std(0)
         for c in range(CAPS):
             normalise(c)
             regroup(c)
             if c + 1 < CAPS:
-                mean_and_std(c + 1)
+                mean_and_rstd(c + 1)
             if c >= 1:
                 multiply_and_store(c - 1, vector_is_idle=False)
             if c + 2 < CAPS:
                 partial_statistics(c + 2)
-            if c + 1 < CAPS:
-                invert_std(c + 1)
             quantise(c)
         multiply_and_store(CAPS - 1, vector_is_idle=True)

@@ -31,14 +31,14 @@ def tile_caps_bn_e_kernel(tc, x, weight_words, weight_scales, bias, out):
     nc = tc.nc
 
     x_view = x.rearrange("n (c p t) h w -> c p n (t h w)", c=CAPS, p=P, t=PACK)
-    out_view = out.rearrange("n (c m p) h w -> c m p n (h w)", c=CAPS, m=M_TILES, p=P)
+    out_view = out.rearrange("n (c m p) h w -> c n p m (h w)", c=CAPS, m=M_TILES, p=P)
 
     with ExitStack() as ctx:
         ctx.enter_context(tc.manual_schedule())
         keep = ctx.enter_context(tc.tile_pool(name="keep", bufs=1))
         small = ctx.enter_context(tc.tile_pool(name="small", bufs=4))
         work = ctx.enter_context(tc.tile_pool(name="work", bufs=2))
-        results = ctx.enter_context(tc.tile_pool(name="results", bufs=24))
+        results = ctx.enter_context(tc.tile_pool(name="results", bufs=6))
         psum_once = ctx.enter_context(tc.psum_pool(name="psum_once", bufs=1))
         psum = ctx.enter_context(tc.psum_pool(name="psum", bufs=6))
 
@@ -60,10 +60,10 @@ def tile_caps_bn_e_kernel(tc, x, weight_words, weight_scales, bias, out):
         def load_x(c):
             nc.sync.dma_start(out=x_all[:, c].rearrange("p n t f -> p n (t f)"), in_=x_view[c])
 
-        def load_w(c):
+        def load_w(s):
             nc.sync.dma_start(
-                out=w_codes[:, c, :],
-                in_=weight_words[c].rearrange("p n t -> p (n t)").bitcast(I32),
+                out=w_codes[:, SHARE * s : SHARE * (s + 1), :],
+                in_=weight_words[SHARE * s : SHARE * (s + 1)].rearrange("c p n t -> p c (n t)").bitcast(I32),
             )
 
         def load_w_scales(s):
@@ -76,12 +76,12 @@ def tile_caps_bn_e_kernel(tc, x, weight_words, weight_scales, bias, out):
         nc.scalar.dma_start(out=bias_rows[0 : CAPS * M_TILES, :], in_=bias.rearrange("(r p) -> r p", p=P))
         load_x(0)
         load_x(1)
-        for c in range(CAPS):
-            if c % SHARE == 0:
-                load_w_scales(c // SHARE)
-            load_w(c)
-            if c + 2 < CAPS:
-                load_x(c + 2)
+        load_x(2)
+        for s in range(CAPS // SHARE):
+            load_w_scales(s)
+            load_w(s)
+            for c in range(SHARE * s + 3, min(SHARE * s + 3 + SHARE, CAPS)):
+                load_x(c)
 
         bias_ps = psum_once.tile([P, P], BF16)
         nc.tensor.transpose(bias_ps[:], bias_rows[:], identity[:])
@@ -146,6 +146,7 @@ def tile_caps_bn_e_kernel(tc, x, weight_words, weight_scales, bias, out):
             )
 
         def multiply_and_store(c, vector_is_idle):
+            result = results.tile([P, M_TILES, COLS], F32, name="result")
             for m in range(M_TILES):
                 o_cols = slice(m * P, (m + 1) * P)
                 acc = psum.tile([P, COLS], F32, name="acc")
@@ -158,13 +159,13 @@ def tile_caps_bn_e_kernel(tc, x, weight_words, weight_scales, bias, out):
                     start=True,
                     stop=True,
                 )
-                result = results.tile([P, COLS], F32, name="result")
                 r = c * M_TILES + m
                 if vector_is_idle and m % 2 == 1:
-                    nc.vector.tensor_scalar_add(out=result[:], in0=acc[:], scalar1=bias_cols[:, r : r + 1])
+                    nc.vector.tensor_scalar_add(out=result[:, m, :], in0=acc[:], scalar1=bias_cols[:, r : r + 1])
                 else:
-                    nc.scalar.activation(out=result[:], in_=acc[:], func=ACT.Identity, bias=bias_cols[:, r : r + 1])
-                nc.sync.dma_start(out=out_view[c, m], in_=result[:].rearrange("p (n f) -> p n f", n=BATCH))
+                    nc.scalar.activation(out=result[:, m, :], in_=acc[:], func=ACT.Identity, bias=bias_cols[:, r : r + 1])
+            for n in range(BATCH):
+                nc.sync.dma_start(out=out_view[c, n], in_=result[:, :, n * PIX : (n + 1) * PIX])
 
         partial_statistics(0)
         mean_and_rstd(0)

@@ -31,6 +31,7 @@ def tile_caps_bn_e_kernel(tc, x, weight_words, weight_scales, bias, out):
     nc = tc.nc
 
     x_view = x.rearrange("n (c p t) h w -> c p n (t h w)", c=CAPS, p=P, t=PACK)
+    x_by_image = x.rearrange("n (c p t) h w -> n p c (t h w)", c=CAPS, p=P, t=PACK)
     out_view = out.rearrange("n (c m p) h w -> c n p m (h w)", c=CAPS, m=M_TILES, p=P)
 
     with ExitStack() as ctx:
@@ -74,14 +75,21 @@ def tile_caps_bn_e_kernel(tc, x, weight_words, weight_scales, bias, out):
                 )
 
         nc.scalar.dma_start(out=bias_rows[0 : CAPS * M_TILES, :], in_=bias.rearrange("(r p) -> r p", p=P))
+        def load_x_images(first, count):
+            for n in range(BATCH):
+                nc.sync.dma_start(
+                    out=x_all[:, first : first + count, n].rearrange("p c t f -> p c (t f)"),
+                    in_=x_by_image[n][:, first : first + count, :],
+                )
+
         load_x(0)
         load_x(1)
-        load_x(2)
+        load_x_images(2, 2)
         for s in range(CAPS // SHARE):
             load_w_scales(s)
             load_w(s)
-            for c in range(SHARE * s + 3, min(SHARE * s + 3 + SHARE, CAPS)):
-                load_x(c)
+            if s + 1 < CAPS // SHARE:
+                load_x_images(SHARE * (s + 1), SHARE)
 
         bias_ps = psum_once.tile([P, P], BF16)
         nc.tensor.transpose(bias_ps[:], bias_rows[:], identity[:])

from contextlib import ExitStack

import concourse.mybir as mybir
from concourse.masks import make_identity

F32 = mybir.dt.float32
BF16 = mybir.dt.bfloat16
I32 = mybir.dt.int32
U32 = mybir.dt.uint32
U8 = mybir.dt.uint8
FP8X4 = mybir.dt.float8_e4m3fn_x4
ALU = mybir.AluOpType
ACT = mybir.ActivationFunctionType

P = 128
PACK = 4
BATCH = 2
CAPS = 16
CH = P * PACK
PIX = 256
COLS = BATCH * PIX
M_TILES = CH // P
EPS = 1e-5
STATS = 6
SHARE = 4

FLOPS = 2 * CAPS * CH * CH * COLS


def tile_caps_bn_e_kernel(tc, x, weight_words, weight_scales, bias, out):
    nc = tc.nc

    x_view = x.rearrange("n (c p t) h w -> c p n (t h w)", c=CAPS, p=P, t=PACK)
    x_by_image = x.rearrange("n (c p t) h w -> n p c (t h w)", c=CAPS, p=P, t=PACK)
    out_view = out.rearrange("n (c m p) h w -> c n p m (h w)", c=CAPS, m=M_TILES, p=P)

    with ExitStack() as ctx:
        ctx.enter_context(tc.manual_schedule())
        keep = ctx.enter_context(tc.tile_pool(name="keep", bufs=1))
        small = ctx.enter_context(tc.tile_pool(name="small", bufs=4))
        work = ctx.enter_context(tc.tile_pool(name="work", bufs=2))
        results = ctx.enter_context(tc.tile_pool(name="results", bufs=6))
        psum_once = ctx.enter_context(tc.psum_pool(name="psum_once", bufs=1))
        psum = ctx.enter_context(tc.psum_pool(name="psum", bufs=6))

        x_all = keep.tile([P, CAPS, BATCH, PACK, PIX], BF16)
        w_codes = keep.tile([P, CAPS, CH], I32, align_bytes=64)
        w_planes = keep.tile([P, CAPS // SHARE, CH], U8, align_bytes=64)
        bias_rows = keep.tile([P, P], BF16)
        identity = keep.tile([P, P], BF16)
        bias_cols = keep.tile([P, CAPS * M_TILES], F32)
        zero_col = keep.tile([P, 1], F32)
        eps_col = keep.tile([P, 1], F32)

        nc.vector.memset(w_planes[:].rearrange("p g n -> p (g n)").bitcast(I32), 0)
        nc.vector.memset(bias_rows[:], 0.0)
        nc.vector.memset(zero_col[:], 0.0)
        nc.vector.tensor_scalar_add(out=eps_col[:], in0=zero_col[:], scalar1=EPS)
        make_identity(nc, identity[:])

        def load_x(c):
            nc.sync.dma_start(out=x_all[:, c].rearrange("p n t f -> p n (t f)"), in_=x_view[c])

        def load_w(s):
            nc.sync.dma_start(
                out=w_codes[:, SHARE * s : SHARE * (s + 1), :],
                in_=weight_words[SHARE * s : SHARE * (s + 1)].rearrange("c p n t -> p c (n t)").bitcast(I32),
            )

        def load_w_scales(s):
            for Q in range(4):
                nc.sync.dma_start(
                    out=w_planes[32 * Q : 32 * Q + 4 * SHARE, s, :].bitcast(I32),
                    in_=weight_scales[SHARE * s : SHARE * (s + 1), 4 * Q : 4 * Q + 4, :].bitcast(I32),
                )

        nc.scalar.dma_start(out=bias_rows[0 : CAPS * M_TILES, :], in_=bias.rearrange("(r p) -> r p", p=P))
        def load_x_images(first, count):
            for n in range(BATCH):
                nc.sync.dma_start(
                    out=x_all[:, first : first + count, n].rearrange("p c t f -> p c (t f)"),
                    in_=x_by_image[n][:, first : first + count, :],
                )

        load_x(0)
        load_x(1)
        load_x_images(2, 2)
        for s in range(CAPS // SHARE):
            load_w_scales(s)
            load_w(s)
            if s + 1 < CAPS // SHARE:
                load_x_images(SHARE * (s + 1), SHARE)

        bias_ps = psum_once.tile([P, P], BF16)
        nc.tensor.transpose(bias_ps[:], bias_rows[:], identity[:])
        nc.scalar.copy(out=bias_cols[:], in_=bias_ps[:, 0 : CAPS * M_TILES])

        stats = {}
        mean_var = {}
        rstd = {}
        xn = {}
        grouped = {}
        codes = {}
        planes = {}

        def partial_statistics(c):
            stats[c] = small.tile([P, PACK, STATS], F32, name="stats")
            for t in range(PACK):
                nc.vector.bn_stats(out=stats[c][:, t, :], in_=x_all[:, c, :, t, :])

        def mean_and_rstd(c):
            mean_var[c] = small.tile([P, PACK, 2], F32, name="mean_var")
            rstd[c] = small.tile([P, PACK], F32, name="rstd")
            for t in range(PACK):
                nc.vector.bn_aggr(out=mean_var[c][:, t, :], in_=stats[c][:, t, :])
            nc.scalar.activation(
                out=rstd[c][:], in_=mean_var[c][:, :, 1], func=ACT.Abs_reciprocal_sqrt, bias=eps_col[:]
            )

        def normalise(c):
            xn[c] = work.tile([P, PACK, COLS], BF16, name="xn")
            for t in range(PACK):
                nc.vector.tensor_scalar(
                    out=xn[c][:, t, :].rearrange("p (n f) -> p n f", n=BATCH),
                    in0=x_all[:, c, :, t, :],
                    scalar1=mean_var[c][:, t, 0:1],
                    scalar2=rstd[c][:, t : t + 1],
                    op0=ALU.subtract,
                    op1=ALU.mult,
                )
            grouped[c] = work.tile([P, COLS, PACK], BF16, name="grouped", align_bytes=64)

        def regroup(c):
            nc.scalar.copy(
                out=grouped[c][:, 0:PIX, :].rearrange("p (c i) t -> p c t i", i=4),
                in_=xn[c][:, :, 0:PIX].rearrange("p t (c i) -> p c t i", i=4),
            )
            nc.gpsimd.tensor_scalar(
                out=grouped[c][:, PIX:COLS, :],
                in0=xn[c][:, :, PIX:COLS].rearrange("p t c -> p c t"),
                scalar1=1.0,
                scalar2=0.0,
                op0=ALU.mult,
                op1=ALU.add,
            )

        def quantise(c):
            codes[c] = work.tile([P, COLS], U32, name="codes", align_bytes=64)
            planes[c] = work.tile([P, COLS], U8, name="planes", align_bytes=64)
            nc.vector.quantize_mx(
                out=codes[c][:].bitcast(FP8X4),
                scales=planes[c][:],
                in_=grouped[c][:].rearrange("p c t -> p (c t)"),
            )

        def multiply_and_store(c, vector_is_idle):
            result = results.tile([P, M_TILES, COLS], F32, name="result")
            for m in range(M_TILES):
                o_cols = slice(m * P, (m + 1) * P)
                acc = psum.tile([P, COLS], F32, name="acc")
                nc.tensor.matmul_mx(
                    out=acc[:],
                    lhsT=w_codes[:, c, o_cols].bitcast(FP8X4),
                    lhsT_scale=w_planes[4 * (c % SHARE) : P, c // SHARE, o_cols],
                    rhs=codes[c][:].bitcast(FP8X4),
                    rhs_scale=planes[c][:],
                    start=True,
                    stop=True,
                )
                r = c * M_TILES + m
                if vector_is_idle and m % 2 == 1:
                    nc.vector.tensor_scalar_add(out=result[:, m, :], in0=acc[:], scalar1=bias_cols[:, r : r + 1])
                else:
                    nc.scalar.activation(out=result[:, m, :], in_=acc[:], func=ACT.Identity, bias=bias_cols[:, r : r + 1])
            for n in range(BATCH):
                nc.sync.dma_start(out=out_view[c, n], in_=result[:, :, n * PIX : (n + 1) * PIX])

        partial_statistics(0)
        mean_and_rstd(0)
        partial_statistics(1)
        for c in range(CAPS):
            normalise(c)
            regroup(c)
            if c + 1 < CAPS:
                mean_and_rstd(c + 1)
            if c >= 1:
                multiply_and_store(c - 1, vector_is_idle=False)
            if c + 2 < CAPS:
                partial_statistics(c + 2)
            quantise(c)
        multiply_and_store(CAPS - 1, vector_is_idle=True)
